import numpy as np
import ml_dtypes


def mxq(x, axis, fmt="e4m3"):
    dtype, down = {"e4m3": (ml_dtypes.float8_e4m3fn, 7), "e5m2": (ml_dtypes.float8_e5m2, 14)}[fmt]
    v = np.moveaxis(np.asarray(x, np.float32).astype(ml_dtypes.bfloat16).astype(np.float64), axis, -1)
    blocks = v.reshape(v.shape[:-1] + (-1, 32))
    amax = np.abs(blocks).max(-1, keepdims=True)
    byte = np.maximum(np.where(amax > 0, np.frexp(amax)[1] - 1 + 127, 0) - down, 1)
    scale = np.exp2(byte - 127.0)
    codes = (blocks / scale).astype(np.float32).astype(dtype).astype(np.float64)
    return np.moveaxis((codes * scale).reshape(v.shape), -1, axis)


WIDE = False


def mx_kscale(k):
    if not WIDE:
        return np.ones(k)
    levels = np.array([10, -10, 5, -5, 0])
    a = np.random.permutation(np.resize(levels, k // 512 * 4)).reshape(k // 512, 4)
    idx = np.arange(k)
    return np.exp2(a[idx // 512, idx % 128 // 32])


BF16 = ml_dtypes.bfloat16


def bf(x):
    return np.asarray(x, np.float32).astype(BF16)


def f64(x):
    return np.asarray(x).astype(np.float64)


B, D, K, STAGES = 16384, 512, 256, 5
EPS = 1e-6


def setup_inputs():
    s = mx_kscale(D)
    p = np.random.standard_normal((K, D))
    p = p / (EPS + np.sqrt((p * p).sum(axis=1, keepdims=True)))
    return {"cls": bf(np.random.standard_normal((B, D)) * 0.5 * s), "proto": bf(p / s)}


def reference(cls, proto):
    x, p = f64(cls), f64(proto)
    dot = mxq(x, 1, "e4m3") @ mxq(p, 1, "e4m3").T
    e = np.exp(dot - dot.max(axis=1, keepdims=True))
    r = e / e.sum(axis=1, keepdims=True)
    m = mxq(r, 0, "e4m3").T @ mxq(x, 0, "e4m3")
    return m / (np.sqrt((m * m).sum(axis=1, keepdims=True)) + EPS)

@@ -1,0 +1,254 @@
+from contextlib import ExitStack
+
+import concourse.mybir as mybir
+from concourse.masks import make_identity
+
+B, D, K = 16384, 512, 256
+FLOPS = 2 * 2 * B * D * K
+
+BF16 = mybir.dt.bfloat16
+F32 = mybir.dt.float32
+U32 = mybir.dt.uint32
+U8 = mybir.dt.uint8
+FP8X4 = mybir.dt.float8_e4m3fn_x4
+ACT = mybir.ActivationFunctionType
+ALU = mybir.AluOpType
+AX = mybir.AxisListType
+
+P = 128
+PACK = 4
+ROWS = P * PACK
+NG = B // ROWS
+GD = 160
+LEAD = 1
+EPS = 1e-6
+
+
+def tile_gmm_pa_t_kernel(tc, cls, proto, out):
+    nc = tc.nc
+    with ExitStack() as ctx:
+        const = ctx.enter_context(tc.tile_pool(name="const", bufs=1))
+        xpool = ctx.enter_context(tc.tile_pool(name="xpool", bufs=NG))
+        g1pool = ctx.enter_context(tc.tile_pool(name="g1pool", bufs=3))
+        c1pool = ctx.enter_context(tc.tile_pool(name="c1pool", bufs=3))
+        stat = ctx.enter_context(tc.tile_pool(name="stat", bufs=3))
+        epool = ctx.enter_context(tc.tile_pool(name="epool", bufs=3))
+        rgpool = ctx.enter_context(tc.tile_pool(name="rgpool", bufs=2))
+        rcpool = ctx.enter_context(tc.tile_pool(name="rcpool", bufs=3))
+        g2pool = ctx.enter_context(tc.tile_pool(name="g2pool", bufs=2))
+        c2pool = ctx.enter_context(tc.tile_pool(name="c2pool", bufs=LEAD + 4))
+        ps_t = ctx.enter_context(tc.psum_pool(name="ps_t", bufs=2))
+        ps_d = ctx.enter_context(tc.psum_pool(name="ps_d", bufs=4))
+        ps_m = ctx.enter_context(tc.psum_pool(name="ps_m", bufs=1))
+        ctx.enter_context(tc.manual_schedule())
+
+        p_raw = const.tile([P, 2, D], BF16, name="p_raw")
+        nc.sync.dma_start(out=p_raw[:], in_=proto.rearrange("(p a) d -> p a d", a=2))
+        x_view = cls.rearrange("(g p j) d -> g p j d", p=P, j=PACK)
+        xs = []
+        for g in range(NG):
+            x_g = xpool.tile([P, PACK, D], BF16, name="x_g")
+            nc.sync.dma_start(out=x_g[:], in_=x_view[g])
+            xs.append(x_g)
+
+        ident = const.tile([P, P], F32, name="ident")
+        make_identity(nc, ident[:])
+        one = const.tile([P, 1], F32, name="one")
+        nc.vector.memset(one[:], 1.0)
+        warm = const.tile([P, 2], F32, name="warm")
+        nc.scalar.activation(out=warm[:, 0:1], in_=one[:], func=ACT.Exp)
+
+        p_w = p_raw[:].bitcast(F32)
+        p_ps = ps_t.tile([P, 2, 2, P], F32, name="t_ps")
+        for a in range(2):
+            for u in range(2):
+                nc.tensor.transpose(out=p_ps[:, a, u, :], in_=p_w[:, a, u * P:(u + 1) * P], identity=ident[:])
+        p_grp = const.tile([P, K, PACK], BF16, name="p_grp", align_bytes=64)
+        nc.vector.tensor_copy(
+            out=p_grp[:].bitcast(F32).rearrange("q (c p) u -> q c p u", c=2),
+            in_=p_ps[:].rearrange("q c u p -> q c p u"),
+        )
+        p_codes = const.tile([P, K], U32, name="p_codes", align_bytes=64)
+        p_scales = const.tile([P, K], U8, name="p_scales", align_bytes=64)
+        nc.vector.quantize_mx(
+            out=p_codes[:].bitcast(FP8X4), scales=p_scales[:], in_=p_grp[:].rearrange("q c t -> q (c t)")
+        )
+
+        m_ps = [ps_m.tile([P, D], F32, name="m_ps%d" % h) for h in range(2)]
+
+        t_banks = {}
+        g1s = {}
+        c1s = {}
+        dots = {}
+        nmaxs = {}
+        sums = {}
+        es = {}
+        rgs = {}
+        rcs = {}
+        g2s = {}
+        c2s = {}
+
+        def transposes(g):
+            x_w = xs[g][:].bitcast(F32)
+            banks = []
+            for a in range(2):
+                t_ps = ps_t.tile([P, 2, 2, P], F32, name="t_ps")
+                for c in range(2):
+                    for u in range(2):
+                        nc.tensor.transpose(
+                            out=t_ps[:, c, u, :], in_=x_w[:, 2 * a + c, u * P:(u + 1) * P], identity=ident[:]
+                        )
+                banks.append(t_ps)
+            t_banks[g] = banks
+
+        def copy_out(g):
+            g1 = g1pool.tile([P, ROWS, PACK], BF16, name="g1", align_bytes=64)
+            g1_w = g1[:].bitcast(F32)
+            for a in range(2):
+                nc.scalar.copy(
+                    out=g1_w[:, a * 2 * P:(a + 1) * 2 * P, :].rearrange("q (c p) u -> q c p u", c=2),
+                    in_=t_banks[g][a][:].rearrange("q c u p -> q c p u"),
+                )
+            g1s[g] = g1
+
+        def quantise_d(g):
+            codes = c1pool.tile([P, ROWS], U32, name="c1_codes", align_bytes=64)
+            scales = c1pool.tile([P, ROWS], U8, name="c1_scales", align_bytes=64)
+            nc.vector.quantize_mx(
+                out=codes[:].bitcast(FP8X4), scales=scales[:], in_=g1s[g][:].rearrange("q c t -> q (c t)")
+            )
+            c1s[g] = (codes, scales)
+
+        def matmul_1(g):
+            codes, scales = c1s[g]
+            banks = []
+            for a in range(2):
+                dot = ps_d.tile([P, 2, K], F32, name="dot")
+                for c in range(2):
+                    cols = slice((2 * a + c) * P, (2 * a + c + 1) * P)
+                    nc.tensor.matmul_mx(
+                        out=dot[:, c, :],
+                        lhsT=codes[:, cols].bitcast(FP8X4),
+                        lhsT_scale=scales[:, cols],
+                        rhs=p_codes[:].bitcast(FP8X4),
+                        rhs_scale=p_scales[:],
+                        start=True,
+                        stop=True,
+                    )
+                banks.append(dot)
+            dots[g] = banks
+
+        def row_max(g):
+            nmax = stat.tile([P, PACK], F32, name="nmax")
+            for a in range(2):
+                nc.vector.tensor_reduce(
+                    out=nmax[:, 2 * a:2 * a + 2], in_=dots[g][a][:], axis=AX.X, op=ALU.max, negate=True
+                )
+            nmaxs[g] = nmax
+
+        def exps(g):
+            e = epool.tile([P, PACK, K], F32, name="e")
+            ssum = stat.tile([P, PACK], F32, name="ssum")
+            for j in range(PACK):
+                nc.scalar.activation(
+                    out=e[:, j, :],
+                    in_=dots[g][j // 2][:, j % 2, :],
+                    func=ACT.Exp,
+                    bias=nmaxs[g][:, j:j + 1],
+                    scale=1.0,
+                    accum_out=ssum[:, j:j + 1],
+                )
+            es[g] = e
+            sums[g] = ssum
+
+        def normalise(g):
+            rs = stat.tile([P, PACK], F32, name="rs")
+            nc.vector.reciprocal(out=rs[:], in_=sums[g][:])
+            rg = rgpool.tile([P, K, PACK], BF16, name="rg", align_bytes=64)
+            nc.vector.tensor_tensor(
+                out=rg[:],
+                in0=es[g][:].rearrange("p j k -> p k j"),
+                in1=rs[:].unsqueeze(1).to_broadcast([P, K, PACK]),
+                op=ALU.mult,
+            )
+            rgs[g] = rg
+
+        def quantise_r(g):
+            codes = rcpool.tile([P, K], U32, name="r_codes", align_bytes=64)
+            scales = rcpool.tile([P, K], U8, name="r_scales", align_bytes=64)
+            nc.vector.quantize_mx(
+                out=codes[:].bitcast(FP8X4), scales=scales[:], in_=rgs[g][:].rearrange("p k j -> p (k j)")
+            )
+            rcs[g] = (codes, scales)
+
+        def regroup(g):
+            g2 = g2pool.tile([P, D, PACK], BF16, name="g2", align_bytes=64)
+            nc.gpsimd.tensor_scalar(
+                out=g2[:, :GD, :],
+                in0=xs[g][:, :, :GD].rearrange("p t c -> p c t"),
+                scalar1=1.0,
+                scalar2=0.0,
+                op0=ALU.mult,
+                op1=ALU.add,
+            )
+            nc.scalar.copy(
+                out=g2[:, GD:, :].rearrange("p (c i) t -> p c t i", i=4),
+                in_=xs[g][:, :, GD:].rearrange("p t (c i) -> p c t i", i=4),
+            )
+            g2s[g] = g2
+
+        def quantise_b(g):
+            codes = c2pool.tile([P, D], U32, name="c2_codes", align_bytes=64)
+            scales = c2pool.tile([P, D], U8, name="c2_scales", align_bytes=64)
+            nc.vector.quantize_mx(
+                out=codes[:].bitcast(FP8X4), scales=scales[:], in_=g2s[g][:].rearrange("p d t -> p (d t)")
+            )
+            c2s[g] = (codes, scales)
+
+        def matmul_2(g):
+            r_codes, r_scales = rcs[g]
+            x_codes, x_scales = c2s[g]
+            for h in range(2):
+                cols = slice(h * P, (h + 1) * P)
+                nc.tensor.matmul_mx(
+                    out=m_ps[h][:],
+                    lhsT=r_codes[:, cols].bitcast(FP8X4),
+                    lhsT_scale=r_scales[:, cols],
+                    rhs=x_codes[:].bitcast(FP8X4),
+                    rhs_scale=x_scales[:],
+                    start=(g == 0),
+                    stop=(g == NG - 1),
+                )
+
+        def run(stage, g):
+            if 0 <= g < NG:
+                stage(g)
+
+        for i in range(-3 - LEAD, NG + 2):
+            run(transposes, i + 3)
+            run(matmul_2, i - 2)
+            run(matmul_1, i + 1)
+            run(row_max, i)
+            run(exps, i)
+            run(copy_out, i + 3)
+            run(normalise, i - 1)
+            run(quantise_d, i + 2)
+            run(quantise_r, i - 1)
+            run(quantise_b, i + LEAD)
+            run(regroup, i + LEAD + 2)
+            if i == NG - 1:
+                nc.scalar.activation(out=warm[:, 1:2], in_=one[:], func=ACT.Sqrt)
+
+        junk = const.tile([P, D], F32, name="junk")
+        ss = const.tile([P, 2], F32, name="ss")
+        for h in range(2):
+            nc.scalar.activation(out=junk[:], in_=m_ps[h][:], func=ACT.Square, accum_out=ss[:, h:h + 1])
+        norm = const.tile([P, 2], F32, name="norm")
+        nc.scalar.activation(out=norm[:], in_=ss[:], func=ACT.Sqrt)
+        inv = const.tile([P, 2], F32, name="inv")
+        nc.vector.tensor_scalar_add(out=inv[:], in0=norm[:], scalar1=EPS)
+        nc.vector.reciprocal(out=inv[:], in_=inv[:])
+        res = const.tile([P, 2, D], F32, name="res")
+        nc.vector.tensor_scalar_mul(out=res[:, 0, :], in0=m_ps[0][:], scalar1=inv[:, 0:1])
+        nc.scalar.activation(out=res[:, 1, :], in_=m_ps[1][:], func=ACT.Copy, scale=inv[:, 1:2])
+        nc.sync.dma_start(out=out.rearrange("(p a) d -> p a d", a=2), in_=res[:])

@@ -166,9 +166,9 @@ def tile_gmm_pa_t_kernel(tc, cls, proto, out):
             nc.vector.reciprocal(out=rs[:], in_=sums[g][:])
             rg = rgpool.tile([P, K, PACK], BF16, name="rg", align_bytes=64)
             nc.vector.tensor_tensor(
-                out=rg[:],
-                in0=es[g][:].rearrange("p j k -> p k j"),
-                in1=rs[:].unsqueeze(1).to_broadcast([P, K, PACK]),
+                out=rg[:].rearrange("p (c i) j -> p c j i", i=4),
+                in0=es[g][:].rearrange("p j (c i) -> p c j i", i=4),
+                in1=rs[:].unsqueeze(1).unsqueeze(3).to_broadcast([P, K // 4, PACK, 4]),
                 op=ALU.mult,
             )
             rgs[g] = rg

@@ -19,7 +19,7 @@ P = 128
 PACK = 4
 ROWS = P * PACK
 NG = B // ROWS
-GD = 160
+GD = 192
 LEAD = 1
 EPS = 1e-6
 

@@ -82,6 +82,7 @@ def tile_gmm_pa_t_kernel(tc, cls, proto, out):
         dots = {}
         nmaxs = {}
         sums = {}
+        rss = {}
         es = {}
         rgs = {}
         rcs = {}
@@ -161,9 +162,13 @@ def tile_gmm_pa_t_kernel(tc, cls, proto, out):
             es[g] = e
             sums[g] = ssum
 
-        def normalise(g):
+        def reciprocals(g):
             rs = stat.tile([P, PACK], F32, name="rs")
             nc.vector.reciprocal(out=rs[:], in_=sums[g][:])
+            rss[g] = rs
+
+        def normalise(g):
+            rs = rss[g]
             rg = rgpool.tile([P, K, PACK], BF16, name="rg", align_bytes=64)
             nc.vector.tensor_tensor(
                 out=rg[:].rearrange("p (c i) j -> p c j i", i=4),
@@ -228,6 +233,7 @@ def tile_gmm_pa_t_kernel(tc, cls, proto, out):
             run(transposes, i + 3)
             run(matmul_2, i - 2)
             run(matmul_1, i + 1)
+            run(reciprocals, i - 1)
             run(row_max, i)
             run(exps, i)
             run(copy_out, i + 3)

@@ -19,7 +19,8 @@ P = 128
 PACK = 4
 ROWS = P * PACK
 NG = B // ROWS
-GD = 192
+GD = 128
+CD = 192
 LEAD = 1
 EPS = 1e-6
 
@@ -38,7 +39,8 @@ def tile_gmm_pa_t_kernel(tc, cls, proto, out):
         g2pool = ctx.enter_context(tc.tile_pool(name="g2pool", bufs=2))
         c2pool = ctx.enter_context(tc.tile_pool(name="c2pool", bufs=LEAD + 4))
         ps_t = ctx.enter_context(tc.psum_pool(name="ps_t", bufs=2))
-        ps_d = ctx.enter_context(tc.psum_pool(name="ps_d", bufs=4))
+        ps_d = ctx.enter_context(tc.psum_pool(name="ps_d", bufs=3))
+        ps_c = ctx.enter_context(tc.psum_pool(name="ps_c", bufs=1))
         ps_m = ctx.enter_context(tc.psum_pool(name="ps_m", bufs=1))
         ctx.enter_context(tc.manual_schedule())
 
@@ -53,6 +55,8 @@ def tile_gmm_pa_t_kernel(tc, cls, proto, out):
 
         ident = const.tile([P, P], F32, name="ident")
         make_identity(nc, ident[:])
+        ident_b = const.tile([P, P], BF16, name="ident_b")
+        make_identity(nc, ident_b[:])
         one = const.tile([P, 1], F32, name="one")
         nc.vector.memset(one[:], 1.0)
         warm = const.tile([P, 2], F32, name="warm")
@@ -87,6 +91,7 @@ def tile_gmm_pa_t_kernel(tc, cls, proto, out):
         rgs = {}
         rcs = {}
         g2s = {}
+        c_banks = {}
         c2s = {}
 
         def transposes(g):
@@ -186,6 +191,18 @@ def tile_gmm_pa_t_kernel(tc, cls, proto, out):
             )
             rcs[g] = (codes, scales)
 
+        def regroup_pe(g):
+            c_ps = ps_c.tile([P, CD, PACK], BF16, name="c_ps")
+            for h in range(2):
+                nc.tensor.matmul(
+                    out=c_ps[:, h * CD // 2:(h + 1) * CD // 2, :],
+                    lhsT=ident_b[:],
+                    rhs=xs[g][:, :, GD + h * CD // 2:GD + (h + 1) * CD // 2].rearrange("p t c -> p c t"),
+                    start=True,
+                    stop=True,
+                )
+            c_banks[g] = c_ps
+
         def regroup(g):
             g2 = g2pool.tile([P, D, PACK], BF16, name="g2", align_bytes=64)
             nc.gpsimd.tensor_scalar(
@@ -196,9 +213,10 @@ def tile_gmm_pa_t_kernel(tc, cls, proto, out):
                 op0=ALU.mult,
                 op1=ALU.add,
             )
+            nc.scalar.copy(out=g2[:, GD:GD + CD, :], in_=c_banks[g][:])
             nc.scalar.copy(
-                out=g2[:, GD:, :].rearrange("p (c i) t -> p c t i", i=4),
-                in_=xs[g][:, :, GD:].rearrange("p t (c i) -> p c t i", i=4),
+                out=g2[:, GD + CD:, :].rearrange("p (c i) t -> p c t i", i=4),
+                in_=xs[g][:, :, GD + CD:].rearrange("p t (c i) -> p c t i", i=4),
             )
             g2s[g] = g2
 
@@ -233,6 +251,7 @@ def tile_gmm_pa_t_kernel(tc, cls, proto, out):
             run(transposes, i + 3)
             run(matmul_2, i - 2)
             run(matmul_1, i + 1)
+            run(regroup_pe, i + LEAD + 2)
             run(reciprocals, i - 1)
             run(row_max, i)
             run(exps, i)

@@ -36,7 +36,7 @@ def tile_gmm_pa_t_kernel(tc, cls, proto, out):
         epool = ctx.enter_context(tc.tile_pool(name="epool", bufs=3))
         rgpool = ctx.enter_context(tc.tile_pool(name="rgpool", bufs=2))
         rcpool = ctx.enter_context(tc.tile_pool(name="rcpool", bufs=3))
-        g2pool = ctx.enter_context(tc.tile_pool(name="g2pool", bufs=2))
+        g2pool = ctx.enter_context(tc.tile_pool(name="g2pool", bufs=3))
         c2pool = ctx.enter_context(tc.tile_pool(name="c2pool", bufs=LEAD + 4))
         ps_t = ctx.enter_context(tc.psum_pool(name="ps_t", bufs=2))
         ps_d = ctx.enter_context(tc.psum_pool(name="ps_d", bufs=3))

@@ -20,8 +20,7 @@ PACK = 4
 ROWS = P * PACK
 NG = B // ROWS
 GD = 128
-CD = 192
-LEAD = 1
+CD = 200
 EPS = 1e-6
 
 
@@ -30,14 +29,12 @@ def tile_gmm_pa_t_kernel(tc, cls, proto, out):
     with ExitStack() as ctx:
         const = ctx.enter_context(tc.tile_pool(name="const", bufs=1))
         xpool = ctx.enter_context(tc.tile_pool(name="xpool", bufs=NG))
-        g1pool = ctx.enter_context(tc.tile_pool(name="g1pool", bufs=3))
-        c1pool = ctx.enter_context(tc.tile_pool(name="c1pool", bufs=3))
         stat = ctx.enter_context(tc.tile_pool(name="stat", bufs=3))
         epool = ctx.enter_context(tc.tile_pool(name="epool", bufs=3))
         rgpool = ctx.enter_context(tc.tile_pool(name="rgpool", bufs=2))
         rcpool = ctx.enter_context(tc.tile_pool(name="rcpool", bufs=3))
-        g2pool = ctx.enter_context(tc.tile_pool(name="g2pool", bufs=3))
-        c2pool = ctx.enter_context(tc.tile_pool(name="c2pool", bufs=LEAD + 4))
+        gpool = ctx.enter_context(tc.tile_pool(name="gpool", bufs=3))
+        xcpool = ctx.enter_context(tc.tile_pool(name="xcpool", bufs=6))
         ps_t = ctx.enter_context(tc.psum_pool(name="ps_t", bufs=2))
         ps_d = ctx.enter_context(tc.psum_pool(name="ps_d", bufs=3))
         ps_c = ctx.enter_context(tc.psum_pool(name="ps_c", bufs=1))
@@ -81,8 +78,8 @@ def tile_gmm_pa_t_kernel(tc, cls, proto, out):
         m_ps = [ps_m.tile([P, D], F32, name="m_ps%d" % h) for h in range(2)]
 
         t_banks = {}
-        g1s = {}
-        c1s = {}
+        gs = {}
+        xcs = {}
         dots = {}
         nmaxs = {}
         sums = {}
@@ -90,9 +87,7 @@ def tile_gmm_pa_t_kernel(tc, cls, proto, out):
         es = {}
         rgs = {}
         rcs = {}
-        g2s = {}
         c_banks = {}
-        c2s = {}
 
         def transposes(g):
             x_w = xs[g][:].bitcast(F32)
@@ -108,25 +103,25 @@ def tile_gmm_pa_t_kernel(tc, cls, proto, out):
             t_banks[g] = banks
 
         def copy_out(g):
-            g1 = g1pool.tile([P, ROWS, PACK], BF16, name="g1", align_bytes=64)
-            g1_w = g1[:].bitcast(F32)
+            grp = gpool.tile([P, 2, ROWS, PACK], BF16, name="grp", align_bytes=64)
+            g1_w = grp[:, 0, :, :].bitcast(F32)
             for a in range(2):
                 nc.scalar.copy(
                     out=g1_w[:, a * 2 * P:(a + 1) * 2 * P, :].rearrange("q (c p) u -> q c p u", c=2),
                     in_=t_banks[g][a][:].rearrange("q c u p -> q c p u"),
                 )
-            g1s[g] = g1
+            gs[g] = grp
 
-        def quantise_d(g):
-            codes = c1pool.tile([P, ROWS], U32, name="c1_codes", align_bytes=64)
-            scales = c1pool.tile([P, ROWS], U8, name="c1_scales", align_bytes=64)
+        def quantise_x(g):
+            codes = xcpool.tile([P, ROWS + D], U32, name="x_codes", align_bytes=64)
+            scales = xcpool.tile([P, ROWS + D], U8, name="x_scales", align_bytes=64)
             nc.vector.quantize_mx(
-                out=codes[:].bitcast(FP8X4), scales=scales[:], in_=g1s[g][:].rearrange("q c t -> q (c t)")
+                out=codes[:].bitcast(FP8X4), scales=scales[:], in_=gs[g][:].rearrange("q h c t -> q (h c t)")
             )
-            c1s[g] = (codes, scales)
+            xcs[g] = (codes, scales)
 
         def matmul_1(g):
-            codes, scales = c1s[g]
+            codes, scales = xcs[g]
             banks = []
             for a in range(2):
                 dot = ps_d.tile([P, 2, K], F32, name="dot")
@@ -204,7 +199,7 @@ def tile_gmm_pa_t_kernel(tc, cls, proto, out):
             c_banks[g] = c_ps
 
         def regroup(g):
-            g2 = g2pool.tile([P, D, PACK], BF16, name="g2", align_bytes=64)
+            g2 = gs[g][:, 1, :, :]
             nc.gpsimd.tensor_scalar(
                 out=g2[:, :GD, :],
                 in0=xs[g][:, :, :GD].rearrange("p t c -> p c t"),
@@ -218,27 +213,18 @@ def tile_gmm_pa_t_kernel(tc, cls, proto, out):
                 out=g2[:, GD + CD:, :].rearrange("p (c i) t -> p c t i", i=4),
                 in_=xs[g][:, :, GD + CD:].rearrange("p t (c i) -> p c t i", i=4),
             )
-            g2s[g] = g2
-
-        def quantise_b(g):
-            codes = c2pool.tile([P, D], U32, name="c2_codes", align_bytes=64)
-            scales = c2pool.tile([P, D], U8, name="c2_scales", align_bytes=64)
-            nc.vector.quantize_mx(
-                out=codes[:].bitcast(FP8X4), scales=scales[:], in_=g2s[g][:].rearrange("p d t -> p (d t)")
-            )
-            c2s[g] = (codes, scales)
 
         def matmul_2(g):
             r_codes, r_scales = rcs[g]
-            x_codes, x_scales = c2s[g]
+            x_codes, x_scales = xcs[g]
             for h in range(2):
                 cols = slice(h * P, (h + 1) * P)
                 nc.tensor.matmul_mx(
                     out=m_ps[h][:],
                     lhsT=r_codes[:, cols].bitcast(FP8X4),
                     lhsT_scale=r_scales[:, cols],
-                    rhs=x_codes[:].bitcast(FP8X4),
-                    rhs_scale=x_scales[:],
+                    rhs=x_codes[:, ROWS:].bitcast(FP8X4),
+                    rhs_scale=x_scales[:, ROWS:],
                     start=(g == 0),
                     stop=(g == NG - 1),
                 )
@@ -247,20 +233,19 @@ def tile_gmm_pa_t_kernel(tc, cls, proto, out):
             if 0 <= g < NG:
                 stage(g)
 
-        for i in range(-3 - LEAD, NG + 2):
+        for i in range(-3, NG + 2):
             run(transposes, i + 3)
             run(matmul_2, i - 2)
             run(matmul_1, i + 1)
-            run(regroup_pe, i + LEAD + 2)
+            run(regroup_pe, i + 3)
             run(reciprocals, i - 1)
             run(row_max, i)
             run(exps, i)
             run(copy_out, i + 3)
             run(normalise, i - 1)
-            run(quantise_d, i + 2)
+            run(quantise_x, i + 2)
             run(quantise_r, i - 1)
-            run(quantise_b, i + LEAD)
-            run(regroup, i + LEAD + 2)
+            run(regroup, i + 3)
             if i == NG - 1:
                 nc.scalar.activation(out=warm[:, 1:2], in_=one[:], func=ACT.Sqrt)
 

@@ -19,7 +19,7 @@ P = 128
 PACK = 4
 ROWS = P * PACK
 NG = B // ROWS
-GD = 128
+GD = 176
 CD = 200
 EPS = 1e-6
 

@@ -21,6 +21,7 @@ ROWS = P * PACK
 NG = B // ROWS
 GD = 176
 CD = 200
+SE = D - CD
 EPS = 1e-6
 
 
@@ -33,7 +34,7 @@ def tile_gmm_pa_t_kernel(tc, cls, proto, out):
         epool = ctx.enter_context(tc.tile_pool(name="epool", bufs=3))
         rgpool = ctx.enter_context(tc.tile_pool(name="rgpool", bufs=2))
         rcpool = ctx.enter_context(tc.tile_pool(name="rcpool", bufs=3))
-        gpool = ctx.enter_context(tc.tile_pool(name="gpool", bufs=3))
+        gpool = ctx.enter_context(tc.tile_pool(name="gpool", bufs=2))
         xcpool = ctx.enter_context(tc.tile_pool(name="xcpool", bufs=6))
         ps_t = ctx.enter_context(tc.psum_pool(name="ps_t", bufs=2))
         ps_d = ctx.enter_context(tc.psum_pool(name="ps_d", bufs=3))
@@ -42,13 +43,14 @@ def tile_gmm_pa_t_kernel(tc, cls, proto, out):
         ctx.enter_context(tc.manual_schedule())
 
         p_raw = const.tile([P, 2, D], BF16, name="p_raw")
-        nc.sync.dma_start(out=p_raw[:], in_=proto.rearrange("(p a) d -> p a d", a=2))
         x_view = cls.rearrange("(g p j) d -> g p j d", p=P, j=PACK)
         xs = []
         for g in range(NG):
             x_g = xpool.tile([P, PACK, D], BF16, name="x_g")
             nc.sync.dma_start(out=x_g[:], in_=x_view[g])
             xs.append(x_g)
+            if g == 0:
+                nc.sync.dma_start(out=p_raw[:], in_=proto.rearrange("(p a) d -> p a d", a=2))
 
         ident = const.tile([P, P], F32, name="ident")
         make_identity(nc, ident[:])
@@ -58,22 +60,6 @@ def tile_gmm_pa_t_kernel(tc, cls, proto, out):
         nc.vector.memset(one[:], 1.0)
         warm = const.tile([P, 2], F32, name="warm")
         nc.scalar.activation(out=warm[:, 0:1], in_=one[:], func=ACT.Exp)
-
-        p_w = p_raw[:].bitcast(F32)
-        p_ps = ps_t.tile([P, 2, 2, P], F32, name="t_ps")
-        for a in range(2):
-            for u in range(2):
-                nc.tensor.transpose(out=p_ps[:, a, u, :], in_=p_w[:, a, u * P:(u + 1) * P], identity=ident[:])
-        p_grp = const.tile([P, K, PACK], BF16, name="p_grp", align_bytes=64)
-        nc.vector.tensor_copy(
-            out=p_grp[:].bitcast(F32).rearrange("q (c p) u -> q c p u", c=2),
-            in_=p_ps[:].rearrange("q c u p -> q c p u"),
-        )
-        p_codes = const.tile([P, K], U32, name="p_codes", align_bytes=64)
-        p_scales = const.tile([P, K], U8, name="p_scales", align_bytes=64)
-        nc.vector.quantize_mx(
-            out=p_codes[:].bitcast(FP8X4), scales=p_scales[:], in_=p_grp[:].rearrange("q c t -> q (c t)")
-        )
 
         m_ps = [ps_m.tile([P, D], F32, name="m_ps%d" % h) for h in range(2)]
 
@@ -102,11 +88,12 @@ def tile_gmm_pa_t_kernel(tc, cls, proto, out):
                 banks.append(t_ps)
             t_banks[g] = banks
 
-        def copy_out(g):
+        def copy_out(g, second=nc.scalar.copy):
             grp = gpool.tile([P, 2, ROWS, PACK], BF16, name="grp", align_bytes=64)
             g1_w = grp[:, 0, :, :].bitcast(F32)
             for a in range(2):
-                nc.scalar.copy(
+                copy = nc.scalar.copy if a == 0 else second
+                copy(
                     out=g1_w[:, a * 2 * P:(a + 1) * 2 * P, :].rearrange("q (c p) u -> q c p u", c=2),
                     in_=t_banks[g][a][:].rearrange("q c u p -> q c p u"),
                 )
@@ -167,23 +154,29 @@ def tile_gmm_pa_t_kernel(tc, cls, proto, out):
             nc.vector.reciprocal(out=rs[:], in_=sums[g][:])
             rss[g] = rs
 
-        def normalise(g):
-            rs = rss[g]
+        def normalise(g, parts=1):
             rg = rgpool.tile([P, K, PACK], BF16, name="rg", align_bytes=64)
-            nc.vector.tensor_tensor(
-                out=rg[:].rearrange("p (c i) j -> p c j i", i=4),
-                in0=es[g][:].rearrange("p j (c i) -> p c j i", i=4),
-                in1=rs[:].unsqueeze(1).unsqueeze(3).to_broadcast([P, K // 4, PACK, 4]),
-                op=ALU.mult,
-            )
+            w = K // parts
+            for h in range(parts):
+                nc.vector.tensor_tensor(
+                    out=rg[:, h * w:(h + 1) * w, :].rearrange("p (c i) j -> p c j i", i=4),
+                    in0=es[g][:, :, h * w:(h + 1) * w].rearrange("p j (c i) -> p c j i", i=4),
+                    in1=rss[g][:].unsqueeze(1).unsqueeze(3).to_broadcast([P, w // 4, PACK, 4]),
+                    op=ALU.mult,
+                )
             rgs[g] = rg
 
-        def quantise_r(g):
+        def quantise_r(g, parts=1):
             codes = rcpool.tile([P, K], U32, name="r_codes", align_bytes=64)
             scales = rcpool.tile([P, K], U8, name="r_scales", align_bytes=64)
-            nc.vector.quantize_mx(
-                out=codes[:].bitcast(FP8X4), scales=scales[:], in_=rgs[g][:].rearrange("p k j -> p (k j)")
-            )
+            w = K // parts
+            for h in range(parts):
+                cols = slice(h * w, (h + 1) * w)
+                nc.vector.quantize_mx(
+                    out=codes[:, cols].bitcast(FP8X4),
+                    scales=scales[:, cols],
+                    in_=rgs[g][:, cols, :].rearrange("p k j -> p (k j)"),
+                )
             rcs[g] = (codes, scales)
 
         def regroup_pe(g):
@@ -192,11 +185,14 @@ def tile_gmm_pa_t_kernel(tc, cls, proto, out):
                 nc.tensor.matmul(
                     out=c_ps[:, h * CD // 2:(h + 1) * CD // 2, :],
                     lhsT=ident_b[:],
-                    rhs=xs[g][:, :, GD + h * CD // 2:GD + (h + 1) * CD // 2].rearrange("p t c -> p c t"),
+                    rhs=xs[g][:, :, SE + h * CD // 2:SE + (h + 1) * CD // 2].rearrange("p t c -> p c t"),
                     start=True,
                     stop=True,
                 )
             c_banks[g] = c_ps
+
+        def regroup_copy(g):
+            nc.scalar.copy(out=gs[g][:, 1, SE:, :], in_=c_banks[g][:])
 
         def regroup(g):
             g2 = gs[g][:, 1, :, :]
@@ -208,10 +204,10 @@ def tile_gmm_pa_t_kernel(tc, cls, proto, out):
                 op0=ALU.mult,
                 op1=ALU.add,
             )
-            nc.scalar.copy(out=g2[:, GD:GD + CD, :], in_=c_banks[g][:])
+            regroup_copy(g)
             nc.scalar.copy(
-                out=g2[:, GD + CD:, :].rearrange("p (c i) t -> p c t i", i=4),
-                in_=xs[g][:, :, GD + CD:].rearrange("p t (c i) -> p c t i", i=4),
+                out=g2[:, GD:SE, :].rearrange("p (c i) t -> p c t i", i=4),
+                in_=xs[g][:, :, GD:SE].rearrange("p t (c i) -> p c t i", i=4),
             )
 
         def matmul_2(g):
@@ -229,36 +225,69 @@ def tile_gmm_pa_t_kernel(tc, cls, proto, out):
                     stop=(g == NG - 1),
                 )
 
-        def run(stage, g):
-            if 0 <= g < NG:
+        def run(stage, g, first=0):
+            if first <= g < NG:
                 stage(g)
 
-        for i in range(-3, NG + 2):
-            run(transposes, i + 3)
-            run(matmul_2, i - 2)
-            run(matmul_1, i + 1)
-            run(regroup_pe, i + 3)
+        transposes(0)
+        p_w = p_raw[:].bitcast(F32)
+        p_ps = ps_d.tile([P, 2, 2, P], F32, name="dot")
+        for a in range(2):
+            for u in range(2):
+                nc.tensor.transpose(out=p_ps[:, a, u, :], in_=p_w[:, a, u * P:(u + 1) * P], identity=ident[:])
+        copy_out(0, second=nc.vector.tensor_copy)
+        p_grp = const.tile([P, K, PACK], BF16, name="p_grp", align_bytes=64)
+        nc.scalar.copy(
+            out=p_grp[:].bitcast(F32).rearrange("q (c p) u -> q c p u", c=2),
+            in_=p_ps[:].rearrange("q c u p -> q c p u"),
+        )
+        regroup_pe(0)
+        regroup_copy(0)
+        nc.vector.tensor_copy(
+            out=gs[0][:, 1, :SE, :].rearrange("p (c i) t -> p c t i", i=4),
+            in_=xs[0][:, :, :SE].rearrange("p t (c i) -> p c t i", i=4),
+        )
+        p_codes = const.tile([P, K], U32, name="p_codes", align_bytes=64)
+        p_scales = const.tile([P, K], U8, name="p_scales", align_bytes=64)
+        nc.vector.quantize_mx(
+            out=p_codes[:].bitcast(FP8X4), scales=p_scales[:], in_=p_grp[:].rearrange("q c t -> q (c t)")
+        )
+
+        for i in range(-1, NG + 2):
+            run(transposes, i + 2)
+            run(regroup_pe, i + 2)
             run(reciprocals, i - 1)
             run(row_max, i)
             run(exps, i)
-            run(copy_out, i + 3)
-            run(normalise, i - 1)
-            run(quantise_x, i + 2)
-            run(quantise_r, i - 1)
-            run(regroup, i + 3)
             if i == NG - 1:
                 nc.scalar.activation(out=warm[:, 1:2], in_=one[:], func=ACT.Sqrt)
+            if i - 2 < NG - 1:
+                run(quantise_r, i - 2)
+            run(quantise_x, i + 1)
+            if i - 1 < NG - 1:
+                run(normalise, i - 1)
+            run(copy_out, i + 2, 1)
+            run(regroup, i + 2, 1)
+            run(matmul_1, i + 1)
+            if i - 2 < NG - 1:
+                run(matmul_2, i - 2)
+        normalise(NG - 1, parts=2)
+        quantise_r(NG - 1, parts=2)
+        matmul_2(NG - 1)
 
+        out_view = out.rearrange("(p a) d -> p a d", a=2)
         junk = const.tile([P, D], F32, name="junk")
-        ss = const.tile([P, 2], F32, name="ss")
         for h in range(2):
-            nc.scalar.activation(out=junk[:], in_=m_ps[h][:], func=ACT.Square, accum_out=ss[:, h:h + 1])
-        norm = const.tile([P, 2], F32, name="norm")
-        nc.scalar.activation(out=norm[:], in_=ss[:], func=ACT.Sqrt)
-        inv = const.tile([P, 2], F32, name="inv")
-        nc.vector.tensor_scalar_add(out=inv[:], in0=norm[:], scalar1=EPS)
-        nc.vector.reciprocal(out=inv[:], in_=inv[:])
-        res = const.tile([P, 2, D], F32, name="res")
-        nc.vector.tensor_scalar_mul(out=res[:, 0, :], in0=m_ps[0][:], scalar1=inv[:, 0:1])
-        nc.scalar.activation(out=res[:, 1, :], in_=m_ps[1][:], func=ACT.Copy, scale=inv[:, 1:2])
-        nc.sync.dma_start(out=out.rearrange("(p a) d -> p a d", a=2), in_=res[:])
+            ss = const.tile([P, 1], F32, name="ss%d" % h)
+            nc.scalar.activation(out=junk[:], in_=m_ps[h][:], func=ACT.Square, accum_out=ss[:])
+            norm = const.tile([P, 1], F32, name="norm%d" % h)
+            nc.scalar.activation(out=norm[:], in_=ss[:], func=ACT.Sqrt)
+            inv = const.tile([P, 1], F32, name="inv%d" % h)
+            nc.vector.tensor_scalar_add(out=inv[:], in0=norm[:], scalar1=EPS)
+            nc.vector.reciprocal(out=inv[:], in_=inv[:])
+            res = const.tile([P, D], F32, name="res%d" % h)
+            if h == 0:
+                nc.vector.tensor_scalar_mul(out=res[:], in0=m_ps[h][:], scalar1=inv[:])
+            else:
+                nc.scalar.activation(out=res[:], in_=m_ps[h][:], func=ACT.Copy, scale=inv[:])
+            nc.sync.dma_start(out=out_view[:, h, :], in_=res[:])

@@ -19,9 +19,10 @@ P = 128
 PACK = 4
 ROWS = P * PACK
 NG = B // ROWS
-GD = 176
+VD = 128
 CD = 200
 SE = D - CD
+GK = 96
 EPS = 1e-6
 
 
@@ -32,7 +33,7 @@ def tile_gmm_pa_t_kernel(tc, cls, proto, out):
         xpool = ctx.enter_context(tc.tile_pool(name="xpool", bufs=NG))
         stat = ctx.enter_context(tc.tile_pool(name="stat", bufs=3))
         epool = ctx.enter_context(tc.tile_pool(name="epool", bufs=3))
-        rgpool = ctx.enter_context(tc.tile_pool(name="rgpool", bufs=2))
+        rgpool = ctx.enter_context(tc.tile_pool(name="rgpool", bufs=3))
         rcpool = ctx.enter_context(tc.tile_pool(name="rcpool", bufs=3))
         gpool = ctx.enter_context(tc.tile_pool(name="gpool", bufs=2))
         xcpool = ctx.enter_context(tc.tile_pool(name="xcpool", bufs=6))
@@ -88,16 +89,22 @@ def tile_gmm_pa_t_kernel(tc, cls, proto, out):
                 banks.append(t_ps)
             t_banks[g] = banks
 
-        def copy_out(g, second=nc.scalar.copy):
+        def regroup_vector(g, width=VD):
             grp = gpool.tile([P, 2, ROWS, PACK], BF16, name="grp", align_bytes=64)
-            g1_w = grp[:, 0, :, :].bitcast(F32)
+            nc.vector.tensor_copy(
+                out=grp[:, 1, :width, :].rearrange("p (c i) t -> p c t i", i=4),
+                in_=xs[g][:, :, :width].rearrange("p t (c i) -> p c t i", i=4),
+            )
+            gs[g] = grp
+
+        def copy_out(g, second=nc.scalar.copy):
+            g1_w = gs[g][:, 0, :, :].bitcast(F32)
             for a in range(2):
                 copy = nc.scalar.copy if a == 0 else second
                 copy(
                     out=g1_w[:, a * 2 * P:(a + 1) * 2 * P, :].rearrange("q (c p) u -> q c p u", c=2),
                     in_=t_banks[g][a][:].rearrange("q c u p -> q c p u"),
                 )
-            gs[g] = grp
 
         def quantise_x(g):
             codes = xcpool.tile([P, ROWS + D], U32, name="x_codes", align_bytes=64)
@@ -154,17 +161,25 @@ def tile_gmm_pa_t_kernel(tc, cls, proto, out):
             nc.vector.reciprocal(out=rs[:], in_=sums[g][:])
             rss[g] = rs
 
-        def normalise(g, parts=1):
-            rg = rgpool.tile([P, K, PACK], BF16, name="rg", align_bytes=64)
-            w = K // parts
-            for h in range(parts):
-                nc.vector.tensor_tensor(
-                    out=rg[:, h * w:(h + 1) * w, :].rearrange("p (c i) j -> p c j i", i=4),
-                    in0=es[g][:, :, h * w:(h + 1) * w].rearrange("p j (c i) -> p c j i", i=4),
-                    in1=rss[g][:].unsqueeze(1).unsqueeze(3).to_broadcast([P, w // 4, PACK, 4]),
-                    op=ALU.mult,
-                )
-            rgs[g] = rg
+        def multiply(g, k0, k1):
+            nc.vector.tensor_tensor(
+                out=rgs[g][:, k0:k1, :].rearrange("p (c i) j -> p c j i", i=4),
+                in0=es[g][:, :, k0:k1].rearrange("p j (c i) -> p c j i", i=4),
+                in1=rss[g][:].unsqueeze(1).unsqueeze(3).to_broadcast([P, (k1 - k0) // 4, PACK, 4]),
+                op=ALU.mult,
+            )
+
+        def multiply_gpsimd(g):
+            rgs[g] = rgpool.tile([P, K, PACK], BF16, name="rg", align_bytes=64)
+            nc.gpsimd.tensor_tensor(
+                out=rgs[g][:, :GK, :],
+                in0=es[g][:, :, :GK].rearrange("p j k -> p k j"),
+                in1=rss[g][:].unsqueeze(1).to_broadcast([P, GK, PACK]),
+                op=ALU.mult,
+            )
+
+        def multiply_vector(g):
+            multiply(g, GK, K)
 
         def quantise_r(g, parts=1):
             codes = rcpool.tile([P, K], U32, name="r_codes", align_bytes=64)
@@ -194,20 +209,11 @@ def tile_gmm_pa_t_kernel(tc, cls, proto, out):
         def regroup_copy(g):
             nc.scalar.copy(out=gs[g][:, 1, SE:, :], in_=c_banks[g][:])
 
-        def regroup(g):
-            g2 = gs[g][:, 1, :, :]
-            nc.gpsimd.tensor_scalar(
-                out=g2[:, :GD, :],
-                in0=xs[g][:, :, :GD].rearrange("p t c -> p c t"),
-                scalar1=1.0,
-                scalar2=0.0,
-                op0=ALU.mult,
-                op1=ALU.add,
-            )
+        def regroup_scalar(g):
             regroup_copy(g)
             nc.scalar.copy(
-                out=g2[:, GD:SE, :].rearrange("p (c i) t -> p c t i", i=4),
-                in_=xs[g][:, :, GD:SE].rearrange("p t (c i) -> p c t i", i=4),
+                out=gs[g][:, 1, VD:SE, :].rearrange("p (c i) t -> p c t i", i=4),
+                in_=xs[g][:, :, VD:SE].rearrange("p t (c i) -> p c t i", i=4),
             )
 
         def matmul_2(g):
@@ -235,6 +241,7 @@ def tile_gmm_pa_t_kernel(tc, cls, proto, out):
         for a in range(2):
             for u in range(2):
                 nc.tensor.transpose(out=p_ps[:, a, u, :], in_=p_w[:, a, u * P:(u + 1) * P], identity=ident[:])
+        regroup_vector(0, width=SE)
         copy_out(0, second=nc.vector.tensor_copy)
         p_grp = const.tile([P, K, PACK], BF16, name="p_grp", align_bytes=64)
         nc.scalar.copy(
@@ -243,37 +250,39 @@ def tile_gmm_pa_t_kernel(tc, cls, proto, out):
         )
         regroup_pe(0)
         regroup_copy(0)
-        nc.vector.tensor_copy(
-            out=gs[0][:, 1, :SE, :].rearrange("p (c i) t -> p c t i", i=4),
-            in_=xs[0][:, :, :SE].rearrange("p t (c i) -> p c t i", i=4),
-        )
         p_codes = const.tile([P, K], U32, name="p_codes", align_bytes=64)
         p_scales = const.tile([P, K], U8, name="p_scales", align_bytes=64)
         nc.vector.quantize_mx(
             out=p_codes[:].bitcast(FP8X4), scales=p_scales[:], in_=p_grp[:].rearrange("q c t -> q (c t)")
         )
 
-        for i in range(-1, NG + 2):
+        for i in range(-1, NG + 1):
             run(transposes, i + 2)
             run(regroup_pe, i + 2)
-            run(reciprocals, i - 1)
             run(row_max, i)
             run(exps, i)
             if i == NG - 1:
                 nc.scalar.activation(out=warm[:, 1:2], in_=one[:], func=ACT.Sqrt)
-            if i - 2 < NG - 1:
-                run(quantise_r, i - 2)
+            run(quantise_r, i - 2)
             run(quantise_x, i + 1)
-            if i - 1 < NG - 1:
-                run(normalise, i - 1)
+            run(regroup_vector, i + 2, 1)
+            if i < NG - 1:
+                run(reciprocals, i)
+                run(multiply_gpsimd, i)
+            if i < NG:
+                run(multiply_vector, i - 1)
+            if i == NG - 1:
+                reciprocals(i)
             run(copy_out, i + 2, 1)
-            run(regroup, i + 2, 1)
+            run(regroup_scalar, i + 2, 1)
             run(matmul_1, i + 1)
-            if i - 2 < NG - 1:
-                run(matmul_2, i - 2)
-        normalise(NG - 1, parts=2)
-        quantise_r(NG - 1, parts=2)
-        matmul_2(NG - 1)
+            run(matmul_2, i - 2)
+        g = NG - 1
+        rgs[g] = rgpool.tile([P, K, PACK], BF16, name="rg", align_bytes=64)
+        multiply(g, 0, K // 2)
+        multiply(g, K // 2, K)
+        quantise_r(g, parts=2)
+        matmul_2(g)
 
         out_view = out.rearrange("(p a) d -> p a d", a=2)
         junk = const.tile([P, D], F32, name="junk")

@@ -19,10 +19,10 @@ P = 128
 PACK = 4
 ROWS = P * PACK
 NG = B // ROWS
-VD = 128
-CD = 200
+VD = 112
+CD = 204
 SE = D - CD
-GK = 96
+GK = 104
 EPS = 1e-6
 
 
@@ -48,10 +48,13 @@ def tile_gmm_pa_t_kernel(tc, cls, proto, out):
         xs = []
         for g in range(NG):
             x_g = xpool.tile([P, PACK, D], BF16, name="x_g")
-            nc.sync.dma_start(out=x_g[:], in_=x_view[g])
-            xs.append(x_g)
             if g == 0:
+                nc.sync.dma_start(out=x_g[:, :2, :], in_=x_view[g, :, :2, :])
+                nc.sync.dma_start(out=x_g[:, 2:, :], in_=x_view[g, :, 2:, :])
                 nc.sync.dma_start(out=p_raw[:], in_=proto.rearrange("(p a) d -> p a d", a=2))
+            else:
+                nc.sync.dma_start(out=x_g[:], in_=x_view[g])
+            xs.append(x_g)
 
         ident = const.tile([P, P], F32, name="ident")
         make_identity(nc, ident[:])
@@ -236,6 +239,7 @@ def tile_gmm_pa_t_kernel(tc, cls, proto, out):
                 stage(g)
 
         transposes(0)
+        regroup_pe(0)
         p_w = p_raw[:].bitcast(F32)
         p_ps = ps_d.tile([P, 2, 2, P], F32, name="dot")
         for a in range(2):
@@ -243,13 +247,13 @@ def tile_gmm_pa_t_kernel(tc, cls, proto, out):
                 nc.tensor.transpose(out=p_ps[:, a, u, :], in_=p_w[:, a, u * P:(u + 1) * P], identity=ident[:])
         regroup_vector(0, width=SE)
         copy_out(0, second=nc.vector.tensor_copy)
+        regroup_copy(0)
+        quantise_x(0)
         p_grp = const.tile([P, K, PACK], BF16, name="p_grp", align_bytes=64)
         nc.scalar.copy(
             out=p_grp[:].bitcast(F32).rearrange("q (c p) u -> q c p u", c=2),
             in_=p_ps[:].rearrange("q c u p -> q c p u"),
         )
-        regroup_pe(0)
-        regroup_copy(0)
         p_codes = const.tile([P, K], U32, name="p_codes", align_bytes=64)
         p_scales = const.tile([P, K], U8, name="p_scales", align_bytes=64)
         nc.vector.quantize_mx(
@@ -264,7 +268,7 @@ def tile_gmm_pa_t_kernel(tc, cls, proto, out):
             if i == NG - 1:
                 nc.scalar.activation(out=warm[:, 1:2], in_=one[:], func=ACT.Sqrt)
             run(quantise_r, i - 2)
-            run(quantise_x, i + 1)
+            run(quantise_x, i + 1, 1)
             run(regroup_vector, i + 2, 1)
             if i < NG - 1:
                 run(reciprocals, i)

from contextlib import ExitStack

import concourse.mybir as mybir
from concourse.masks import make_identity

B, D, K = 16384, 512, 256
FLOPS = 2 * 2 * B * D * K

BF16 = mybir.dt.bfloat16
F32 = mybir.dt.float32
U32 = mybir.dt.uint32
U8 = mybir.dt.uint8
FP8X4 = mybir.dt.float8_e4m3fn_x4
ACT = mybir.ActivationFunctionType
ALU = mybir.AluOpType
AX = mybir.AxisListType

P = 128
PACK = 4
ROWS = P * PACK
NG = B // ROWS
VD = 112
CD = 204
SE = D - CD
GK = 104
EPS = 1e-6


def tile_gmm_pa_t_kernel(tc, cls, proto, out):
    nc = tc.nc
    with ExitStack() as ctx:
        const = ctx.enter_context(tc.tile_pool(name="const", bufs=1))
        xpool = ctx.enter_context(tc.tile_pool(name="xpool", bufs=NG))
        stat = ctx.enter_context(tc.tile_pool(name="stat", bufs=3))
        epool = ctx.enter_context(tc.tile_pool(name="epool", bufs=3))
        rgpool = ctx.enter_context(tc.tile_pool(name="rgpool", bufs=3))
        rcpool = ctx.enter_context(tc.tile_pool(name="rcpool", bufs=3))
        gpool = ctx.enter_context(tc.tile_pool(name="gpool", bufs=2))
        xcpool = ctx.enter_context(tc.tile_pool(name="xcpool", bufs=6))
        ps_t = ctx.enter_context(tc.psum_pool(name="ps_t", bufs=2))
        ps_d = ctx.enter_context(tc.psum_pool(name="ps_d", bufs=3))
        ps_c = ctx.enter_context(tc.psum_pool(name="ps_c", bufs=1))
        ps_m = ctx.enter_context(tc.psum_pool(name="ps_m", bufs=1))
        ctx.enter_context(tc.manual_schedule())

        p_raw = const.tile([P, 2, D], BF16, name="p_raw")
        x_view = cls.rearrange("(g p j) d -> g p j d", p=P, j=PACK)
        xs = []
        for g in range(NG):
            x_g = xpool.tile([P, PACK, D], BF16, name="x_g")
            if g == 0:
                nc.sync.dma_start(out=x_g[:, :2, :], in_=x_view[g, :, :2, :])
                nc.sync.dma_start(out=x_g[:, 2:, :], in_=x_view[g, :, 2:, :])
                nc.sync.dma_start(out=p_raw[:], in_=proto.rearrange("(p a) d -> p a d", a=2))
            else:
                nc.sync.dma_start(out=x_g[:], in_=x_view[g])
            xs.append(x_g)

        ident = const.tile([P, P], F32, name="ident")
        make_identity(nc, ident[:])
        ident_b = const.tile([P, P], BF16, name="ident_b")
        make_identity(nc, ident_b[:])
        one = const.tile([P, 1], F32, name="one")
        nc.vector.memset(one[:], 1.0)
        warm = const.tile([P, 2], F32, name="warm")
        nc.scalar.activation(out=warm[:, 0:1], in_=one[:], func=ACT.Exp)

        m_ps = [ps_m.tile([P, D], F32, name="m_ps%d" % h) for h in range(2)]

        t_banks = {}
        gs = {}
        xcs = {}
        dots = {}
        nmaxs = {}
        sums = {}
        rss = {}
        es = {}
        rgs = {}
        rcs = {}
        c_banks = {}

        def transposes(g):
            x_w = xs[g][:].bitcast(F32)
            banks = []
            for a in range(2):
                t_ps = ps_t.tile([P, 2, 2, P], F32, name="t_ps")
                for c in range(2):
                    for u in range(2):
                        nc.tensor.transpose(
                            out=t_ps[:, c, u, :], in_=x_w[:, 2 * a + c, u * P:(u + 1) * P], identity=ident[:]
                        )
                banks.append(t_ps)
            t_banks[g] = banks

        def regroup_vector(g, width=VD):
            grp = gpool.tile([P, 2, ROWS, PACK], BF16, name="grp", align_bytes=64)
            nc.vector.tensor_copy(
                out=grp[:, 1, :width, :].rearrange("p (c i) t -> p c t i", i=4),
                in_=xs[g][:, :, :width].rearrange("p t (c i) -> p c t i", i=4),
            )
            gs[g] = grp

        def copy_out(g, second=nc.scalar.copy):
            g1_w = gs[g][:, 0, :, :].bitcast(F32)
            for a in range(2):
                copy = nc.scalar.copy if a == 0 else second
                copy(
                    out=g1_w[:, a * 2 * P:(a + 1) * 2 * P, :].rearrange("q (c p) u -> q c p u", c=2),
                    in_=t_banks[g][a][:].rearrange("q c u p -> q c p u"),
                )

        def quantise_x(g):
            codes = xcpool.tile([P, ROWS + D], U32, name="x_codes", align_bytes=64)
            scales = xcpool.tile([P, ROWS + D], U8, name="x_scales", align_bytes=64)
            nc.vector.quantize_mx(
                out=codes[:].bitcast(FP8X4), scales=scales[:], in_=gs[g][:].rearrange("q h c t -> q (h c t)")
            )
            xcs[g] = (codes, scales)

        def matmul_1(g):
            codes, scales = xcs[g]
            banks = []
            for a in range(2):
                dot = ps_d.tile([P, 2, K], F32, name="dot")
                for c in range(2):
                    cols = slice((2 * a + c) * P, (2 * a + c + 1) * P)
                    nc.tensor.matmul_mx(
                        out=dot[:, c, :],
                        lhsT=codes[:, cols].bitcast(FP8X4),
                        lhsT_scale=scales[:, cols],
                        rhs=p_codes[:].bitcast(FP8X4),
                        rhs_scale=p_scales[:],
                        start=True,
                        stop=True,
                    )
                banks.append(dot)
            dots[g] = banks

        def row_max(g):
            nmax = stat.tile([P, PACK], F32, name="nmax")
            for a in range(2):
                nc.vector.tensor_reduce(
                    out=nmax[:, 2 * a:2 * a + 2], in_=dots[g][a][:], axis=AX.X, op=ALU.max, negate=True
                )
            nmaxs[g] = nmax

        def exps(g):
            e = epool.tile([P, PACK, K], F32, name="e")
            ssum = stat.tile([P, PACK], F32, name="ssum")
            for j in range(PACK):
                nc.scalar.activation(
                    out=e[:, j, :],
                    in_=dots[g][j // 2][:, j % 2, :],
                    func=ACT.Exp,
                    bias=nmaxs[g][:, j:j + 1],
                    scale=1.0,
                    accum_out=ssum[:, j:j + 1],
                )
            es[g] = e
            sums[g] = ssum

        def reciprocals(g):
            rs = stat.tile([P, PACK], F32, name="rs")
            nc.vector.reciprocal(out=rs[:], in_=sums[g][:])
            rss[g] = rs

        def multiply(g, k0, k1):
            nc.vector.tensor_tensor(
                out=rgs[g][:, k0:k1, :].rearrange("p (c i) j -> p c j i", i=4),
                in0=es[g][:, :, k0:k1].rearrange("p j (c i) -> p c j i", i=4),
                in1=rss[g][:].unsqueeze(1).unsqueeze(3).to_broadcast([P, (k1 - k0) // 4, PACK, 4]),
                op=ALU.mult,
            )

        def multiply_gpsimd(g):
            rgs[g] = rgpool.tile([P, K, PACK], BF16, name="rg", align_bytes=64)
            nc.gpsimd.tensor_tensor(
                out=rgs[g][:, :GK, :],
                in0=es[g][:, :, :GK].rearrange("p j k -> p k j"),
                in1=rss[g][:].unsqueeze(1).to_broadcast([P, GK, PACK]),
                op=ALU.mult,
            )

        def multiply_vector(g):
            multiply(g, GK, K)

        def quantise_r(g, parts=1):
            codes = rcpool.tile([P, K], U32, name="r_codes", align_bytes=64)
            scales = rcpool.tile([P, K], U8, name="r_scales", align_bytes=64)
            w = K // parts
            for h in range(parts):
                cols = slice(h * w, (h + 1) * w)
                nc.vector.quantize_mx(
                    out=codes[:, cols].bitcast(FP8X4),
                    scales=scales[:, cols],
                    in_=rgs[g][:, cols, :].rearrange("p k j -> p (k j)"),
                )
            rcs[g] = (codes, scales)

        def regroup_pe(g):
            c_ps = ps_c.tile([P, CD, PACK], BF16, name="c_ps")
            for h in range(2):
                nc.tensor.matmul(
                    out=c_ps[:, h * CD // 2:(h + 1) * CD // 2, :],
                    lhsT=ident_b[:],
                    rhs=xs[g][:, :, SE + h * CD // 2:SE + (h + 1) * CD // 2].rearrange("p t c -> p c t"),
                    start=True,
                    stop=True,
                )
            c_banks[g] = c_ps

        def regroup_copy(g):
            nc.scalar.copy(out=gs[g][:, 1, SE:, :], in_=c_banks[g][:])

        def regroup_scalar(g):
            regroup_copy(g)
            nc.scalar.copy(
                out=gs[g][:, 1, VD:SE, :].rearrange("p (c i) t -> p c t i", i=4),
                in_=xs[g][:, :, VD:SE].rearrange("p t (c i) -> p c t i", i=4),
            )

        def matmul_2(g):
            r_codes, r_scales = rcs[g]
            x_codes, x_scales = xcs[g]
            for h in range(2):
                cols = slice(h * P, (h + 1) * P)
                nc.tensor.matmul_mx(
                    out=m_ps[h][:],
                    lhsT=r_codes[:, cols].bitcast(FP8X4),
                    lhsT_scale=r_scales[:, cols],
                    rhs=x_codes[:, ROWS:].bitcast(FP8X4),
                    rhs_scale=x_scales[:, ROWS:],
                    start=(g == 0),
                    stop=(g == NG - 1),
                )

        def run(stage, g, first=0):
            if first <= g < NG:
                stage(g)

        transposes(0)
        regroup_pe(0)
        p_w = p_raw[:].bitcast(F32)
        p_ps = ps_d.tile([P, 2, 2, P], F32, name="dot")
        for a in range(2):
            for u in range(2):
                nc.tensor.transpose(out=p_ps[:, a, u, :], in_=p_w[:, a, u * P:(u + 1) * P], identity=ident[:])
        regroup_vector(0, width=SE)
        copy_out(0, second=nc.vector.tensor_copy)
        regroup_copy(0)
        quantise_x(0)
        p_grp = const.tile([P, K, PACK], BF16, name="p_grp", align_bytes=64)
        nc.scalar.copy(
            out=p_grp[:].bitcast(F32).rearrange("q (c p) u -> q c p u", c=2),
            in_=p_ps[:].rearrange("q c u p -> q c p u"),
        )
        p_codes = const.tile([P, K], U32, name="p_codes", align_bytes=64)
        p_scales = const.tile([P, K], U8, name="p_scales", align_bytes=64)
        nc.vector.quantize_mx(
            out=p_codes[:].bitcast(FP8X4), scales=p_scales[:], in_=p_grp[:].rearrange("q c t -> q (c t)")
        )

        for i in range(-1, NG + 1):
            run(transposes, i + 2)
            run(regroup_pe, i + 2)
            run(row_max, i)
            run(exps, i)
            if i == NG - 1:
                nc.scalar.activation(out=warm[:, 1:2], in_=one[:], func=ACT.Sqrt)
            run(quantise_r, i - 2)
            run(quantise_x, i + 1, 1)
            run(regroup_vector, i + 2, 1)
            if i < NG - 1:
                run(reciprocals, i)
                run(multiply_gpsimd, i)
            if i < NG:
                run(multiply_vector, i - 1)
            if i == NG - 1:
                reciprocals(i)
            run(copy_out, i + 2, 1)
            run(regroup_scalar, i + 2, 1)
            run(matmul_1, i + 1)
            run(matmul_2, i - 2)
        g = NG - 1
        rgs[g] = rgpool.tile([P, K, PACK], BF16, name="rg", align_bytes=64)
        multiply(g, 0, K // 2)
        multiply(g, K // 2, K)
        quantise_r(g, parts=2)
        matmul_2(g)

        out_view = out.rearrange("(p a) d -> p a d", a=2)
        junk = const.tile([P, D], F32, name="junk")
        for h in range(2):
            ss = const.tile([P, 1], F32, name="ss%d" % h)
            nc.scalar.activation(out=junk[:], in_=m_ps[h][:], func=ACT.Square, accum_out=ss[:])
            norm = const.tile([P, 1], F32, name="norm%d" % h)
            nc.scalar.activation(out=norm[:], in_=ss[:], func=ACT.Sqrt)
            inv = const.tile([P, 1], F32, name="inv%d" % h)
            nc.vector.tensor_scalar_add(out=inv[:], in0=norm[:], scalar1=EPS)
            nc.vector.reciprocal(out=inv[:], in_=inv[:])
            res = const.tile([P, D], F32, name="res%d" % h)
            if h == 0:
                nc.vector.tensor_scalar_mul(out=res[:], in0=m_ps[h][:], scalar1=inv[:])
            else:
                nc.scalar.activation(out=res[:], in_=m_ps[h][:], func=ACT.Copy, scale=inv[:])
            nc.sync.dma_start(out=out_view[:, h, :], in_=res[:])
